import numpy as np
import ml_dtypes


def mxq(x, axis, fmt="e4m3"):
    dtype, down = {"e4m3": (ml_dtypes.float8_e4m3fn, 7), "e5m2": (ml_dtypes.float8_e5m2, 14)}[fmt]
    v = np.moveaxis(np.asarray(x, np.float32).astype(ml_dtypes.bfloat16).astype(np.float64), axis, -1)
    blocks = v.reshape(v.shape[:-1] + (-1, 32))
    amax = np.abs(blocks).max(-1, keepdims=True)
    byte = np.maximum(np.where(amax > 0, np.frexp(amax)[1] - 1 + 127, 0) - down, 1)
    scale = np.exp2(byte - 127.0)
    codes = (blocks / scale).astype(np.float32).astype(dtype).astype(np.float64)
    return np.moveaxis((codes * scale).reshape(v.shape), -1, axis)


WIDE = False


def mx_kscale(k):
    if not WIDE:
        return np.ones(k)
    levels = np.array([10, -10, 5, -5, 0])
    a = np.random.permutation(np.resize(levels, k // 512 * 4)).reshape(k // 512, 4)
    idx = np.arange(k)
    return np.exp2(a[idx // 512, idx % 128 // 32])


BF16 = ml_dtypes.bfloat16


def bf(x):
    return np.asarray(x, np.float32).astype(BF16)


def f64(x):
    return np.asarray(x).astype(np.float64)


E2M1 = np.array([0.0, 0.5, 1.0, 1.5, 2.0, 3.0, 4.0, 6.0, -0.0, -0.5, -1.0, -1.5, -2.0, -3.0, -4.0, -6.0])


def pack_weight(w, fmt):
    k, n = w.shape
    w = f64(bf(w)).reshape(k // 32, 32, n)
    amax = np.abs(w).max(1)
    if fmt == "e4m3":
        byte = np.frexp(amax)[1] - 1 + 127 - 7
    else:
        mant, ex = np.frexp(amax / 6.0)
        byte = np.where(mant > 0.5, ex, ex - 1) + 127
    byte = np.clip(np.where(amax > 0, byte, 1), 1, 254)
    scaled = (w * np.exp2(127.0 - byte)[:, None, :]).reshape(k, n).astype(np.float32)
    by_word = np.ascontiguousarray(scaled.reshape(k // 512, 128, 4, n).transpose(0, 1, 3, 2))
    if fmt == "e4m3":
        words = by_word.astype(ml_dtypes.float8_e4m3fn).view(np.uint8)
    else:
        c = by_word.astype(ml_dtypes.float4_e2m1fn).view(np.uint8) & 0xF
        words = c[..., 0::2] | (c[..., 1::2] << 4)
    return np.ascontiguousarray(words), np.ascontiguousarray(byte.astype(np.uint8).reshape(k // 512, 16, n))


def unpack_weight(words, scales, fmt):
    g, p, n, _ = words.shape
    if fmt == "e4m3":
        vals = np.ascontiguousarray(words).view(ml_dtypes.float8_e4m3fn).astype(np.float64)
    else:
        nib = np.empty((g, p, n, 4), np.uint8)
        nib[..., 0::2] = words & 0xF
        nib[..., 1::2] = words >> 4
        vals = E2M1[nib]
    vals = vals * np.repeat(np.exp2(scales.astype(np.float64) - 127.0), 8, axis=1)[..., None]
    return vals.transpose(0, 1, 3, 2).reshape(g * 512, n)

def pack4(w):
    words, scales = pack_weight(w, "e2m1")
    return words.reshape(words.shape[0], 128, -1), scales


def unpack4(words, scales):
    return unpack_weight(words.reshape(words.shape[0], 128, -1, 2), scales, "e2m1")


B, U, I, H = 128, 2, 4096, 768


def sigmoid(v):
    return 1.0 / (1.0 + np.exp(-v))


def setup_inputs():
    s = mx_kscale(I)
    inputs = bf(np.random.standard_normal((B, U, I)) * s)
    hidden = bf(np.random.standard_normal((B, U, H)))
    w_ih = np.random.standard_normal((U, 3 * H, I)) / np.sqrt(I) / s
    cat = np.ascontiguousarray(w_ih.swapaxes(1, 2)).reshape(-1, 3 * H)
    words, scales = pack4(cat)
    w_hh = bf(np.random.standard_normal((U, 3 * H, H)) / np.sqrt(H))
    b_ih = bf(np.random.standard_normal((U, 3 * H)) * 0.3)
    b_hh = bf(np.random.standard_normal((U, 3 * H)) * 0.3)
    return {"inputs": inputs,
            "hidden": hidden,
            "w_ih_words": words,
            "w_ih_scales": scales,
            "w_hh": w_hh,
            "b_ih": b_ih,
            "b_hh": b_hh}


def reference(inputs, hidden, w_ih_words, w_ih_scales, w_hh, b_ih, b_hh):
    h = f64(hidden)
    gx = (mxq(f64(inputs), 2, "e4m3").transpose(1, 0, 2) @ unpack4(w_ih_words, w_ih_scales).reshape(U, I, 3 * H)).transpose(1, 0, 2) + f64(b_ih)
    gh = (h.transpose(1, 0, 2) @ f64(w_hh).transpose(0, 2, 1)).transpose(1, 0, 2) + f64(b_hh)
    xr, xz, xn = gx[..., :H], gx[..., H:2 * H], gx[..., 2 * H:]
    hr, hz, hn = gh[..., :H], gh[..., H:2 * H], gh[..., 2 * H:]
    r = sigmoid(xr + hr)
    z = sigmoid(xz + hz)
    n = np.tanh(xn + r * hn)
    return (1.0 - z) * n + z * h

@@ -1,0 +1,310 @@
+from contextlib import ExitStack
+
+import concourse.mybir as mybir
+from concourse.masks import make_identity
+
+F32 = mybir.dt.float32
+BF16 = mybir.dt.bfloat16
+I32 = mybir.dt.int32
+U8 = mybir.dt.uint8
+U32 = mybir.dt.uint32
+FP8X4 = mybir.dt.float8_e4m3fn_x4
+FP4X4 = mybir.dt.float4_e2m1fn_x4
+SIGMOID = mybir.ActivationFunctionType.Sigmoid
+TANH = mybir.ActivationFunctionType.Tanh
+
+P = 128
+U = 2
+I = 4096
+H = 768
+GATES = 3 * H
+K_PASS = 512
+PASSES = I // K_PASS
+BANK = 512
+NARROW = 128
+
+W_CHUNKS = U * GATES // BANK
+ROWS_PER_PART = BANK // P
+PAIR_BLOCKS = H // (2 * P)
+CHUNKS_BEFORE_SCALES = 5
+
+FLOPS = 2 * P * U * GATES * (I + H)
+
+
+def tile_grouptorchgru_w_e_kernel(tc, inputs, hidden, w_ih_words, w_ih_scales, w_hh, b_ih, b_hh, out):
+    nc = tc.nc
+    with ExitStack() as ctx:
+        keep = ctx.enter_context(tc.tile_pool(name="keep", bufs=1))
+        w_rows_pool = ctx.enter_context(tc.tile_pool(name="w_rows", bufs=6))
+        w_cols_pool = ctx.enter_context(tc.tile_pool(name="w_cols", bufs=3))
+        grouped_pool = ctx.enter_context(tc.tile_pool(name="grouped", bufs=2))
+        words_pool = ctx.enter_context(tc.tile_pool(name="words", bufs=6))
+        gate_pool = ctx.enter_context(tc.tile_pool(name="gate", bufs=1))
+        psum = ctx.enter_context(tc.psum_pool(name="psum", bufs=8))
+
+        ident_f32 = keep.tile([P, P], F32)
+        make_identity(nc, ident_f32[:])
+        ident_bf16 = keep.tile([P, P], BF16)
+        make_identity(nc, ident_bf16[:])
+
+        ones = keep.tile([P, P], BF16)
+        nc.vector.memset(ones[:], 1.0)
+        bias_rows = keep.tile([P, U * GATES], BF16)
+        nc.vector.memset(bias_rows[:].bitcast(I32), 0)
+        bias_new_rows = keep.tile([P, U * H], BF16)
+        nc.vector.memset(bias_new_rows[:].bitcast(I32), 0)
+        planes = []
+        for u in range(U):
+            plane = keep.tile([P, PASSES, GATES], U8, name="plane%d" % u, align_bytes=64)
+            nc.vector.memset(plane[:].bitcast(I32), 0)
+            planes.append(plane)
+
+        warm = keep.tile([P, 1], F32)
+        nc.scalar.activation(out=warm[:], in_=ones[:, 0:1], func=SIGMOID)
+
+        hidden_sb = keep.tile([P, U, H], BF16)
+        hidden_t = keep.tile([P, U, 2 * PAIR_BLOCKS, P], BF16)
+        gh_sb = keep.tile([P, U * GATES], F32)
+        bias_new_sb = keep.tile([P, U * H], F32)
+        x_sb = keep.tile([P, U, I], BF16)
+        x_codes = keep.tile([P, U * PASSES, P], U32, align_bytes=64)
+        x_scales = keep.tile([P, U * PASSES, P], U8, align_bytes=64)
+
+        ctx.enter_context(tc.manual_schedule())
+
+        nc.scalar.dma_start(out=bias_rows[0:1, :], in_=b_hh.rearrange("u n -> (u n)").unsqueeze(0))
+        nc.scalar.dma_start(
+            out=bias_rows[1:2, :].rearrange("o (u n) -> o u n", u=U)[:, :, 0 : 2 * H],
+            in_=b_ih.unsqueeze(0)[:, :, 0 : 2 * H],
+        )
+        nc.scalar.dma_start(
+            out=bias_new_rows[0:1, :].rearrange("o (u n) -> o u n", u=U),
+            in_=b_ih.unsqueeze(0)[:, :, 2 * H : 3 * H],
+        )
+
+        w_flat = w_hh.flatten_outer_dims()
+        w_rows = []
+
+        def load_w_chunk(c):
+            rows = w_rows_pool.tile([P, ROWS_PER_PART, H], BF16, name="rows%d" % c, tag="rows")
+            nc.sync.dma_start(
+                out=rows[:],
+                in_=w_flat[BANK * c : BANK * (c + 1), :].rearrange("(p j) k -> p j k", j=ROWS_PER_PART),
+            )
+            w_rows.append(rows)
+
+        scale_rows = w_ih_scales.bitcast(I32).rearrange("g q c -> q g c")
+
+        def load_scales(u):
+            plane = planes[u][:].bitcast(I32)
+            for half in range(2):
+                local = slice(4 * half, 4 * half + 4)
+                given = slice(PASSES * u + 4 * half, PASSES * u + 4 * half + 4)
+                for b in range(2):
+                    for r in range(4):
+                        nc.sync.dma_start(
+                            out=plane[32 * b + r : P : 64, local, :],
+                            in_=scale_rows[4 * b + r : 16 : 8, given, :],
+                        )
+
+        words_i32 = w_ih_words.bitcast(I32)
+
+        def load_words(first_pass, n_passes, first_col, n_cols, name):
+            tile_u8 = words_pool.tile([P, n_passes * n_cols * 2], U8, name=name, tag="words", align_bytes=64)
+            nc.sync.dma_start(
+                out=tile_u8[:].bitcast(I32).rearrange("p (g c) -> p g c", g=n_passes),
+                in_=words_i32[
+                    first_pass : first_pass + n_passes, :, first_col // 2 : (first_col + n_cols) // 2
+                ].rearrange("g p c -> p g c"),
+            )
+            return tile_u8
+
+        nc.sync.dma_start(out=hidden_sb[:], in_=hidden)
+        for c in range(CHUNKS_BEFORE_SCALES):
+            load_w_chunk(c)
+        load_scales(0)
+        for c in range(CHUNKS_BEFORE_SCALES, W_CHUNKS):
+            load_w_chunk(c)
+        for u in range(U):
+            nc.sync.dma_start(out=x_sb[:, u, :], in_=inputs[:, u, :])
+        load_scales(1)
+        rz_words = []
+        new_words = []
+        for u in range(U):
+            rz_words.append(
+                [load_words(PASSES * u + 2 * i, 2, 0, 2 * H, "rz%d_%d" % (u, i)) for i in range(PASSES // 2)]
+            )
+            new_words.append(
+                [load_words(PASSES * u + 4 * i, 4, 2 * H, H, "nw%d_%d" % (u, i)) for i in range(PASSES // 4)]
+            )
+
+        for u in range(U):
+            h_bank = psum.tile([P, 2 * BANK], BF16, name="h_bank", tag="bank")
+            for s in range(2 * PAIR_BLOCKS):
+                kb, e = divmod(s, 2)
+                nc.tensor.transpose(
+                    h_bank[:, P * s : P * (s + 1)],
+                    hidden_sb[:, u, 2 * P * kb + e : 2 * P * (kb + 1) : 2],
+                    ident_bf16[:],
+                )
+            nc.scalar.copy(
+                out=hidden_t[:, u, :, :].rearrange("p s b -> p (s b)"), in_=h_bank[:, 0 : 2 * PAIR_BLOCKS * P]
+            )
+
+        def transpose_w_chunk(c):
+            pairs = w_rows[c][:].bitcast(F32)
+            cols = w_cols_pool.tile([P, PAIR_BLOCKS, BANK], F32, name="cols%d" % c, tag="cols")
+            for kb in range(PAIR_BLOCKS):
+                bank = psum.tile([P, BANK], F32, name="w_bank", tag="bank")
+                for j in range(ROWS_PER_PART):
+                    nc.tensor.transpose(
+                        bank[:, P * j : P * (j + 1)], pairs[:, j, P * kb : P * (kb + 1)], ident_f32[:]
+                    )
+                nc.vector.tensor_copy(
+                    out=cols[:, kb, :].rearrange("p (r j) -> p r j", j=ROWS_PER_PART),
+                    in_=bank[:].rearrange("p (j r) -> p r j", j=ROWS_PER_PART),
+                )
+            return cols
+
+        def units_in_chunk(c):
+            pieces = []
+            for u in range(U):
+                lo = max(BANK * c, GATES * u)
+                hi = min(BANK * (c + 1), GATES * (u + 1))
+                if lo < hi:
+                    pieces.append((u, lo - BANK * c, hi - BANK * c))
+            return pieces
+
+        def multiply_w_chunk(c, cols):
+            halves = cols[:].bitcast(BF16).rearrange("p k (n e) -> p k n e", e=2)
+            acc = psum.tile([P, BANK], F32, name="gh_bank", tag="bank")
+            for u, lo, hi in units_in_chunk(c):
+                for s in range(2 * PAIR_BLOCKS):
+                    kb, e = divmod(s, 2)
+                    nc.tensor.matmul(
+                        out=acc[:, lo:hi],
+                        lhsT=hidden_t[:, u, s, :],
+                        rhs=halves[:, kb, lo:hi, e],
+                        start=(s == 0),
+                        stop=False,
+                    )
+                nc.tensor.matmul(
+                    out=acc[:, lo:hi],
+                    lhsT=ones[:],
+                    rhs=bias_rows[:, BANK * c + lo : BANK * c + hi],
+                    start=False,
+                    stop=True,
+                )
+            nc.scalar.copy(out=gh_sb[:, BANK * c : BANK * (c + 1)], in_=acc[:])
+
+        w_cols = [transpose_w_chunk(0)]
+        for c in range(1, W_CHUNKS):
+            w_cols.append(transpose_w_chunk(c))
+            multiply_w_chunk(c - 1, w_cols[c - 1])
+        multiply_w_chunk(W_CHUNKS - 1, w_cols[W_CHUNKS - 1])
+
+        def quantise_inputs(u):
+            pairs = x_sb[:, u, :].bitcast(F32)
+            staged = []
+            for q in range(2):
+                grouped = grouped_pool.tile([P, 4 * K_PASS], BF16, name="grouped", tag="grouped", align_bytes=64)
+                grouped_pairs = grouped[:].bitcast(F32)
+                for h in range(2):
+                    bank = psum.tile([P, BANK], F32, name="x_bank", tag="bank")
+                    for g2 in range(2):
+                        g = 4 * q + 2 * h + g2
+                        for w in range(2):
+                            nc.tensor.transpose(
+                                bank[:, P * (2 * g2 + w) : P * (2 * g2 + w + 1)],
+                                pairs[:, 2 * P * g + w : 2 * P * (g + 1) : 2],
+                                ident_f32[:],
+                            )
+                    dst = grouped_pairs[:, BANK * h : BANK * (h + 1)].rearrange("p (g b w) -> p g b w", g=2, w=2)
+                    src = bank[:].rearrange("p (g w b) -> p g b w", g=2, w=2)
+                    if h == 0:
+                        nc.scalar.copy(out=dst, in_=src)
+                    else:
+                        nc.vector.tensor_copy(out=dst, in_=src)
+                staged.append(grouped)
+            for q in range(2):
+                four = slice(PASSES * u + 4 * q, PASSES * u + 4 * q + 4)
+                nc.vector.quantize_mx(
+                    out=x_codes[:, four, :].rearrange("p g b -> p (g b)").bitcast(FP8X4),
+                    scales=x_scales[:, four, :].rearrange("p g b -> p (g b)"),
+                    in_=staged[q][:],
+                )
+
+        def spread_new_bias():
+            for i in range(U * H // BANK):
+                acc = psum.tile([P, BANK], F32, name="bias_bank", tag="bank")
+                nc.tensor.matmul(
+                    out=acc[:], lhsT=ones[:], rhs=bias_new_rows[:, BANK * i : BANK * (i + 1)], start=True, stop=True
+                )
+                nc.scalar.copy(out=bias_new_sb[:, BANK * i : BANK * (i + 1)], in_=acc[:])
+
+        quantise_inputs(0)
+        spread_new_bias()
+        quantise_inputs(1)
+
+        def mx_pass(acc, u, g, words, first_col, width):
+            nc.tensor.matmul_mx(
+                out=acc,
+                lhsT=x_codes[:, PASSES * u + g, :].bitcast(FP8X4),
+                lhsT_scale=x_scales[:, PASSES * u + g, :],
+                rhs=words.bitcast(FP4X4),
+                rhs_scale=planes[u][:, g, first_col : first_col + width],
+                start=(g == 0),
+                stop=(g == PASSES - 1),
+            )
+
+        for u in range(U):
+            gh_u = gh_sb[:, GATES * u : GATES * (u + 1)]
+
+            rz_acc = [psum.tile([P, BANK], F32, name="rz_bank%d" % i, tag="bank") for i in range(2 * H // BANK)]
+            for g in range(PASSES):
+                words = rz_words[u][g // 2]
+                for i in range(2 * H // BANK):
+                    start_byte = 2 * (2 * H * (g % 2) + BANK * i)
+                    mx_pass(rz_acc[i][:], u, g, words[:, start_byte : start_byte + 2 * BANK], BANK * i, BANK)
+
+            pre = gate_pool.tile([P, 2 * H], F32, name="pre")
+            for i in range(2 * H // BANK):
+                cols = slice(BANK * i, BANK * (i + 1))
+                nc.vector.tensor_add(out=pre[:, cols], in0=rz_acc[i][:], in1=gh_u[:, cols])
+            reset = gate_pool.tile([P, H], F32, name="reset")
+            update = gate_pool.tile([P, H], F32, name="update")
+            keep_new = gate_pool.tile([P, H], F32, name="keep_new")
+            nc.scalar.activation(out=reset[:], in_=pre[:, 0:H], func=SIGMOID)
+            nc.scalar.activation(out=update[:], in_=pre[:, H : 2 * H], func=SIGMOID)
+            nc.scalar.activation(out=keep_new[:], in_=pre[:, H : 2 * H], func=SIGMOID, scale=-1.0)
+            cand = gate_pool.tile([P, H], F32, name="cand")
+            nc.vector.tensor_mul(out=cand[:], in0=reset[:], in1=gh_u[:, 2 * H : 3 * H])
+            nc.vector.tensor_add(out=cand[:], in0=cand[:], in1=bias_new_sb[:, H * u : H * (u + 1)])
+            old_part = gate_pool.tile([P, H], F32, name="old_part")
+            nc.vector.tensor_mul(out=old_part[:], in0=update[:], in1=hidden_sb[:, u, :])
+
+            widths = [BANK, NARROW, NARROW]
+            starts = [0, BANK, BANK + NARROW]
+            new_acc = [psum.tile([P, BANK], F32, name="new_bank%d" % i, tag="bank") for i in range(3)]
+            for g in range(PASSES):
+                words = new_words[u][g // 4]
+                for i in range(3):
+                    start_byte = 2 * (H * (g % 4) + starts[i])
+                    mx_pass(
+                        new_acc[i][:, 0 : widths[i]],
+                        u,
+                        g,
+                        words[:, start_byte : start_byte + 2 * widths[i]],
+                        2 * H + starts[i],
+                        widths[i],
+                    )
+
+            for i in range(3):
+                cols = slice(starts[i], starts[i] + widths[i])
+                nc.vector.tensor_add(out=cand[:, cols], in0=new_acc[i][:, 0 : widths[i]], in1=cand[:, cols])
+            result = gate_pool.tile([P, H], F32, name="result")
+            for cols in (slice(0, BANK), slice(BANK, H)):
+                nc.scalar.activation(out=cand[:, cols], in_=cand[:, cols], func=TANH)
+                nc.vector.tensor_mul(out=result[:, cols], in0=cand[:, cols], in1=keep_new[:, cols])
+                nc.vector.tensor_add(out=result[:, cols], in0=result[:, cols], in1=old_part[:, cols])
+                nc.sync.dma_start(out=out[:, u, cols], in_=result[:, cols])

@@ -26,7 +26,7 @@ NARROW = 128
 W_CHUNKS = U * GATES // BANK
 ROWS_PER_PART = BANK // P
 PAIR_BLOCKS = H // (2 * P)
-CHUNKS_BEFORE_SCALES = 5
+PASSES_PER_DMA = 2
 
 FLOPS = 2 * P * U * GATES * (I + H)
 
@@ -111,23 +111,25 @@ def tile_grouptorchgru_w_e_kernel(tc, inputs, hidden, w_ih_words, w_ih_scales, w
 
         def load_words(first_pass, n_passes, first_col, n_cols, name):
             tile_u8 = words_pool.tile([P, n_passes * n_cols * 2], U8, name=name, tag="words", align_bytes=64)
-            nc.sync.dma_start(
-                out=tile_u8[:].bitcast(I32).rearrange("p (g c) -> p g c", g=n_passes),
-                in_=words_i32[
-                    first_pass : first_pass + n_passes, :, first_col // 2 : (first_col + n_cols) // 2
-                ].rearrange("g p c -> p g c"),
-            )
+            by_pass = tile_u8[:].bitcast(I32).rearrange("p (g c) -> p g c", g=n_passes)
+            for g in range(0, n_passes, PASSES_PER_DMA):
+                nc.sync.dma_start(
+                    out=by_pass[:, g : g + PASSES_PER_DMA, :],
+                    in_=words_i32[
+                        first_pass + g : first_pass + g + PASSES_PER_DMA,
+                        :,
+                        first_col // 2 : (first_col + n_cols) // 2,
+                    ].rearrange("g p c -> p g c"),
+                )
             return tile_u8
 
         nc.sync.dma_start(out=hidden_sb[:], in_=hidden)
-        for c in range(CHUNKS_BEFORE_SCALES):
-            load_w_chunk(c)
-        load_scales(0)
-        for c in range(CHUNKS_BEFORE_SCALES, W_CHUNKS):
+        for c in range(W_CHUNKS):
             load_w_chunk(c)
         for u in range(U):
             nc.sync.dma_start(out=x_sb[:, u, :], in_=inputs[:, u, :])
-        load_scales(1)
+        for u in range(U):
+            load_scales(u)
         rz_words = []
         new_words = []
         for u in range(U):
@@ -151,20 +153,27 @@ def tile_grouptorchgru_w_e_kernel(tc, inputs, hidden, w_ih_words, w_ih_scales, w
                 out=hidden_t[:, u, :, :].rearrange("p s b -> p (s b)"), in_=h_bank[:, 0 : 2 * PAIR_BLOCKS * P]
             )
 
-        def transpose_w_chunk(c):
+        w_cols = []
+        w_banks = []
+
+        def transpose_two(c, s):
+            kb, half = divmod(s, 2)
+            if s == 0:
+                w_cols.append(w_cols_pool.tile([P, PAIR_BLOCKS, BANK], F32, name="cols%d" % c, tag="cols"))
+                w_banks.append([])
+            if half == 0:
+                w_banks[c].append(psum.tile([P, BANK], F32, name="w_bank", tag="bank"))
+            bank = w_banks[c][kb]
             pairs = w_rows[c][:].bitcast(F32)
-            cols = w_cols_pool.tile([P, PAIR_BLOCKS, BANK], F32, name="cols%d" % c, tag="cols")
-            for kb in range(PAIR_BLOCKS):
-                bank = psum.tile([P, BANK], F32, name="w_bank", tag="bank")
-                for j in range(ROWS_PER_PART):
-                    nc.tensor.transpose(
-                        bank[:, P * j : P * (j + 1)], pairs[:, j, P * kb : P * (kb + 1)], ident_f32[:]
-                    )
-                nc.vector.tensor_copy(
-                    out=cols[:, kb, :].rearrange("p (r j) -> p r j", j=ROWS_PER_PART),
-                    in_=bank[:].rearrange("p (j r) -> p r j", j=ROWS_PER_PART),
-                )
-            return cols
+            for j in (2 * half, 2 * half + 1):
+                nc.tensor.transpose(bank[:, P * j : P * (j + 1)], pairs[:, j, P * kb : P * (kb + 1)], ident_f32[:])
+            if half == 1:
+                dst = w_cols[c][:, kb, :].rearrange("p (r j) -> p r j", j=ROWS_PER_PART)
+                src = bank[:].rearrange("p (j r) -> p r j", j=ROWS_PER_PART)
+                if kb == 1:
+                    nc.scalar.copy(out=dst, in_=src)
+                else:
+                    nc.vector.tensor_copy(out=dst, in_=src)
 
         def units_in_chunk(c):
             pieces = []
@@ -175,10 +184,10 @@ def tile_grouptorchgru_w_e_kernel(tc, inputs, hidden, w_ih_words, w_ih_scales, w
                     pieces.append((u, lo - BANK * c, hi - BANK * c))
             return pieces
 
-        def multiply_w_chunk(c, cols):
-            halves = cols[:].bitcast(BF16).rearrange("p k (n e) -> p k n e", e=2)
+        def multiply_w_chunk(c):
+            halves = w_cols[c][:].bitcast(BF16).rearrange("p k (n e) -> p k n e", e=2)
             acc = psum.tile([P, BANK], F32, name="gh_bank", tag="bank")
-            for u, lo, hi in units_in_chunk(c):
+            for piece, (u, lo, hi) in enumerate(units_in_chunk(c)):
                 for s in range(2 * PAIR_BLOCKS):
                     kb, e = divmod(s, 2)
                     nc.tensor.matmul(
@@ -188,6 +197,8 @@ def tile_grouptorchgru_w_e_kernel(tc, inputs, hidden, w_ih_words, w_ih_scales, w
                         start=(s == 0),
                         stop=False,
                     )
+                    if piece == 0 and c + 1 < W_CHUNKS:
+                        transpose_two(c + 1, s)
                 nc.tensor.matmul(
                     out=acc[:, lo:hi],
                     lhsT=ones[:],
@@ -197,11 +208,10 @@ def tile_grouptorchgru_w_e_kernel(tc, inputs, hidden, w_ih_words, w_ih_scales, w
                 )
             nc.scalar.copy(out=gh_sb[:, BANK * c : BANK * (c + 1)], in_=acc[:])
 
-        w_cols = [transpose_w_chunk(0)]
-        for c in range(1, W_CHUNKS):
-            w_cols.append(transpose_w_chunk(c))
-            multiply_w_chunk(c - 1, w_cols[c - 1])
-        multiply_w_chunk(W_CHUNKS - 1, w_cols[W_CHUNKS - 1])
+        for s in range(2 * PAIR_BLOCKS):
+            transpose_two(0, s)
+        for c in range(W_CHUNKS):
+            multiply_w_chunk(c)
 
         def quantise_inputs(u):
             pairs = x_sb[:, u, :].bitcast(F32)

@@ -26,7 +26,7 @@ NARROW = 128
 W_CHUNKS = U * GATES // BANK
 ROWS_PER_PART = BANK // P
 PAIR_BLOCKS = H // (2 * P)
-PASSES_PER_DMA = 2
+GROUPS = ((0, 1024, 2), (1024, 512, 4), (1536, 512, 4), (2048, 256, 4))
 
 FLOPS = 2 * P * U * GATES * (I + H)
 
@@ -38,7 +38,7 @@ def tile_grouptorchgru_w_e_kernel(tc, inputs, hidden, w_ih_words, w_ih_scales, w
         w_rows_pool = ctx.enter_context(tc.tile_pool(name="w_rows", bufs=6))
         w_cols_pool = ctx.enter_context(tc.tile_pool(name="w_cols", bufs=3))
         grouped_pool = ctx.enter_context(tc.tile_pool(name="grouped", bufs=2))
-        words_pool = ctx.enter_context(tc.tile_pool(name="words", bufs=6))
+        words_pool = ctx.enter_context(tc.tile_pool(name="words", bufs=9))
         gate_pool = ctx.enter_context(tc.tile_pool(name="gate", bufs=1))
         psum = ctx.enter_context(tc.psum_pool(name="psum", bufs=8))
 
@@ -109,19 +109,23 @@ def tile_grouptorchgru_w_e_kernel(tc, inputs, hidden, w_ih_words, w_ih_scales, w
 
         words_i32 = w_ih_words.bitcast(I32)
 
-        def load_words(first_pass, n_passes, first_col, n_cols, name):
-            tile_u8 = words_pool.tile([P, n_passes * n_cols * 2], U8, name=name, tag="words", align_bytes=64)
-            by_pass = tile_u8[:].bitcast(I32).rearrange("p (g c) -> p g c", g=n_passes)
-            for g in range(0, n_passes, PASSES_PER_DMA):
+        def load_words(u, group):
+            first_col, n_cols, n_passes = GROUPS[group]
+            tiles = []
+            for first_pass in range(0, PASSES, n_passes):
+                tile_u8 = words_pool.tile(
+                    [P, n_passes * n_cols * 2], U8, name="w%d_%d_%d" % (u, group, first_pass), tag="words", align_bytes=64
+                )
                 nc.sync.dma_start(
-                    out=by_pass[:, g : g + PASSES_PER_DMA, :],
+                    out=tile_u8[:].bitcast(I32).rearrange("p (g c) -> p g c", g=n_passes),
                     in_=words_i32[
-                        first_pass + g : first_pass + g + PASSES_PER_DMA,
+                        PASSES * u + first_pass : PASSES * u + first_pass + n_passes,
                         :,
                         first_col // 2 : (first_col + n_cols) // 2,
                     ].rearrange("g p c -> p g c"),
                 )
-            return tile_u8
+                tiles.append(tile_u8)
+            return tiles
 
         nc.sync.dma_start(out=hidden_sb[:], in_=hidden)
         for c in range(W_CHUNKS):
@@ -130,15 +134,7 @@ def tile_grouptorchgru_w_e_kernel(tc, inputs, hidden, w_ih_words, w_ih_scales, w
             nc.sync.dma_start(out=x_sb[:, u, :], in_=inputs[:, u, :])
         for u in range(U):
             load_scales(u)
-        rz_words = []
-        new_words = []
-        for u in range(U):
-            rz_words.append(
-                [load_words(PASSES * u + 2 * i, 2, 0, 2 * H, "rz%d_%d" % (u, i)) for i in range(PASSES // 2)]
-            )
-            new_words.append(
-                [load_words(PASSES * u + 4 * i, 4, 2 * H, H, "nw%d_%d" % (u, i)) for i in range(PASSES // 4)]
-            )
+        words = [[load_words(u, group) for group in range(len(GROUPS))] for u in range(U)]
 
         for u in range(U):
             h_bank = psum.tile([P, 2 * BANK], BF16, name="h_bank", tag="bank")
@@ -267,54 +263,65 @@ def tile_grouptorchgru_w_e_kernel(tc, inputs, hidden, w_ih_words, w_ih_scales, w
                 stop=(g == PASSES - 1),
             )
 
+        def multiply_group(u, group):
+            first_col, n_cols, n_passes = GROUPS[group]
+            width = min(n_cols, BANK) if n_cols >= BANK else NARROW
+            accs = [
+                psum.tile([P, BANK], F32, name="acc%d_%d" % (group, i), tag="bank") for i in range(n_cols // width)
+            ]
+            for g in range(PASSES):
+                tile_u8 = words[u][group][g // n_passes]
+                for i in range(n_cols // width):
+                    start_byte = 2 * (n_cols * (g % n_passes) + width * i)
+                    mx_pass(
+                        accs[i][:, 0:width],
+                        u,
+                        g,
+                        tile_u8[:, start_byte : start_byte + 2 * width],
+                        first_col + width * i,
+                        width,
+                    )
+            return accs
+
         for u in range(U):
             gh_u = gh_sb[:, GATES * u : GATES * (u + 1)]
-
-            rz_acc = [psum.tile([P, BANK], F32, name="rz_bank%d" % i, tag="bank") for i in range(2 * H // BANK)]
-            for g in range(PASSES):
-                words = rz_words[u][g // 2]
-                for i in range(2 * H // BANK):
-                    start_byte = 2 * (2 * H * (g % 2) + BANK * i)
-                    mx_pass(rz_acc[i][:], u, g, words[:, start_byte : start_byte + 2 * BANK], BANK * i, BANK)
-
             pre = gate_pool.tile([P, 2 * H], F32, name="pre")
-            for i in range(2 * H // BANK):
-                cols = slice(BANK * i, BANK * (i + 1))
-                nc.vector.tensor_add(out=pre[:, cols], in0=rz_acc[i][:], in1=gh_u[:, cols])
             reset = gate_pool.tile([P, H], F32, name="reset")
             update = gate_pool.tile([P, H], F32, name="update")
             keep_new = gate_pool.tile([P, H], F32, name="keep_new")
+            cand = gate_pool.tile([P, H], F32, name="cand")
+            old_part = gate_pool.tile([P, H], F32, name="old_part")
+            result = gate_pool.tile([P, H], F32, name="result")
+
+            accs = multiply_group(u, 0)
+            for i in range(2):
+                cols = slice(BANK * i, BANK * (i + 1))
+                nc.vector.tensor_add(out=pre[:, cols], in0=accs[i][:], in1=gh_u[:, cols])
             nc.scalar.activation(out=reset[:], in_=pre[:, 0:H], func=SIGMOID)
+
+            accs = multiply_group(u, 1)
+            cols = slice(2 * BANK, 3 * BANK)
+            nc.vector.tensor_add(out=pre[:, cols], in0=accs[0][:], in1=gh_u[:, cols])
             nc.scalar.activation(out=update[:], in_=pre[:, H : 2 * H], func=SIGMOID)
             nc.scalar.activation(out=keep_new[:], in_=pre[:, H : 2 * H], func=SIGMOID, scale=-1.0)
-            cand = gate_pool.tile([P, H], F32, name="cand")
             nc.vector.tensor_mul(out=cand[:], in0=reset[:], in1=gh_u[:, 2 * H : 3 * H])
-            nc.vector.tensor_add(out=cand[:], in0=cand[:], in1=bias_new_sb[:, H * u : H * (u + 1)])
-            old_part = gate_pool.tile([P, H], F32, name="old_part")
             nc.vector.tensor_mul(out=old_part[:], in0=update[:], in1=hidden_sb[:, u, :])
+            nc.vector.tensor_add(out=cand[:], in0=cand[:], in1=bias_new_sb[:, H * u : H * (u + 1)])
 
-            widths = [BANK, NARROW, NARROW]
-            starts = [0, BANK, BANK + NARROW]
-            new_acc = [psum.tile([P, BANK], F32, name="new_bank%d" % i, tag="bank") for i in range(3)]
-            for g in range(PASSES):
-                words = new_words[u][g // 4]
-                for i in range(3):
-                    start_byte = 2 * (H * (g % 4) + starts[i])
-                    mx_pass(
-                        new_acc[i][:, 0 : widths[i]],
-                        u,
-                        g,
-                        words[:, start_byte : start_byte + 2 * widths[i]],
-                        2 * H + starts[i],
-                        widths[i],
-                    )
+            head = slice(0, BANK)
+            tail = slice(BANK, H)
+            accs = multiply_group(u, 2)
+            nc.vector.tensor_add(out=cand[:, head], in0=accs[0][:], in1=cand[:, head])
+            nc.scalar.activation(out=cand[:, head], in_=cand[:, head], func=TANH)
 
-            for i in range(3):
-                cols = slice(starts[i], starts[i] + widths[i])
-                nc.vector.tensor_add(out=cand[:, cols], in0=new_acc[i][:, 0 : widths[i]], in1=cand[:, cols])
-            result = gate_pool.tile([P, H], F32, name="result")
-            for cols in (slice(0, BANK), slice(BANK, H)):
-                nc.scalar.activation(out=cand[:, cols], in_=cand[:, cols], func=TANH)
-                nc.vector.tensor_mul(out=result[:, cols], in0=cand[:, cols], in1=keep_new[:, cols])
-                nc.vector.tensor_add(out=result[:, cols], in0=result[:, cols], in1=old_part[:, cols])
-                nc.sync.dma_start(out=out[:, u, cols], in_=result[:, cols])
+            accs = multiply_group(u, 3)
+            nc.vector.tensor_mul(out=result[:, head], in0=cand[:, head], in1=keep_new[:, head])
+            for i in range(2):
+                cols = slice(BANK + NARROW * i, BANK + NARROW * (i + 1))
+                nc.vector.tensor_add(out=cand[:, cols], in0=accs[i][:, 0:NARROW], in1=cand[:, cols])
+            nc.scalar.activation(out=cand[:, tail], in_=cand[:, tail], func=TANH)
+            nc.vector.tensor_add(out=result[:, head], in0=result[:, head], in1=old_part[:, head])
+            nc.sync.dma_start(out=out[:, u, head], in_=result[:, head])
+            nc.vector.tensor_mul(out=result[:, tail], in0=cand[:, tail], in1=keep_new[:, tail])
+            nc.vector.tensor_add(out=result[:, tail], in0=result[:, tail], in1=old_part[:, tail])
+            nc.sync.dma_start(out=out[:, u, tail], in_=result[:, tail])

@@ -26,7 +26,7 @@ NARROW = 128
 W_CHUNKS = U * GATES // BANK
 ROWS_PER_PART = BANK // P
 PAIR_BLOCKS = H // (2 * P)
-GROUPS = ((0, 1024, 2), (1024, 512, 4), (1536, 512, 4), (2048, 256, 4))
+GROUPS = ((0, 512, 4), (512, 512, 4), (1024, 512, 4), (1536, 512, 4), (2048, 256, 4))
 
 FLOPS = 2 * P * U * GATES * (I + H)
 
@@ -285,36 +285,57 @@ def tile_grouptorchgru_w_e_kernel(tc, inputs, hidden, w_ih_words, w_ih_scales, w
 
         for u in range(U):
             gh_u = gh_sb[:, GATES * u : GATES * (u + 1)]
+            gh_new = gh_u[:, 2 * H : 3 * H]
+            bias_new = bias_new_sb[:, H * u : H * (u + 1)]
             pre = gate_pool.tile([P, 2 * H], F32, name="pre")
-            reset = gate_pool.tile([P, H], F32, name="reset")
-            update = gate_pool.tile([P, H], F32, name="update")
+            gates = gate_pool.tile([P, 2 * H], F32, name="gates")
             keep_new = gate_pool.tile([P, H], F32, name="keep_new")
             cand = gate_pool.tile([P, H], F32, name="cand")
             old_part = gate_pool.tile([P, H], F32, name="old_part")
             result = gate_pool.tile([P, H], F32, name="result")
 
+            def add_hidden_part(group, acc):
+                cols = slice(BANK * group, BANK * (group + 1))
+                nc.vector.tensor_add(out=pre[:, cols], in0=acc[:], in1=gh_u[:, cols])
+                nc.scalar.activation(out=gates[:, cols], in_=pre[:, cols], func=SIGMOID)
+
+            def keep_new_part(lo, hi):
+                nc.scalar.activation(out=keep_new[:, lo:hi], in_=pre[:, H + lo : H + hi], func=SIGMOID, scale=-1.0)
+
+            def cand_part(lo, hi):
+                nc.vector.tensor_mul(out=cand[:, lo:hi], in0=gates[:, lo:hi], in1=gh_new[:, lo:hi])
+
+            def cand_bias_part(lo, hi):
+                nc.vector.tensor_add(out=cand[:, lo:hi], in0=cand[:, lo:hi], in1=bias_new[:, lo:hi])
+
+            def old_part_part(lo, hi):
+                nc.vector.tensor_mul(out=old_part[:, lo:hi], in0=gates[:, H + lo : H + hi], in1=hidden_sb[:, u, lo:hi])
+
+            split = 2 * BANK - H
             accs = multiply_group(u, 0)
-            for i in range(2):
-                cols = slice(BANK * i, BANK * (i + 1))
-                nc.vector.tensor_add(out=pre[:, cols], in0=accs[i][:], in1=gh_u[:, cols])
-            nc.scalar.activation(out=reset[:], in_=pre[:, 0:H], func=SIGMOID)
+            add_hidden_part(0, accs[0])
 
             accs = multiply_group(u, 1)
-            cols = slice(2 * BANK, 3 * BANK)
-            nc.vector.tensor_add(out=pre[:, cols], in0=accs[0][:], in1=gh_u[:, cols])
-            nc.scalar.activation(out=update[:], in_=pre[:, H : 2 * H], func=SIGMOID)
-            nc.scalar.activation(out=keep_new[:], in_=pre[:, H : 2 * H], func=SIGMOID, scale=-1.0)
-            nc.vector.tensor_mul(out=cand[:], in0=reset[:], in1=gh_u[:, 2 * H : 3 * H])
-            nc.vector.tensor_mul(out=old_part[:], in0=update[:], in1=hidden_sb[:, u, :])
-            nc.vector.tensor_add(out=cand[:], in0=cand[:], in1=bias_new_sb[:, H * u : H * (u + 1)])
+            add_hidden_part(1, accs[0])
+            keep_new_part(0, split)
+            cand_part(0, BANK)
+
+            accs = multiply_group(u, 2)
+            add_hidden_part(2, accs[0])
+            keep_new_part(split, H)
+            cand_part(BANK, H)
+            cand_bias_part(0, BANK)
+            old_part_part(0, split)
+            cand_bias_part(BANK, H)
 
             head = slice(0, BANK)
             tail = slice(BANK, H)
-            accs = multiply_group(u, 2)
+            accs = multiply_group(u, 3)
             nc.vector.tensor_add(out=cand[:, head], in0=accs[0][:], in1=cand[:, head])
             nc.scalar.activation(out=cand[:, head], in_=cand[:, head], func=TANH)
+            old_part_part(split, H)
 
-            accs = multiply_group(u, 3)
+            accs = multiply_group(u, 4)
             nc.vector.tensor_mul(out=result[:, head], in0=cand[:, head], in1=keep_new[:, head])
             for i in range(2):
                 cols = slice(BANK + NARROW * i, BANK + NARROW * (i + 1))

@@ -26,7 +26,10 @@ NARROW = 128
 W_CHUNKS = U * GATES // BANK
 ROWS_PER_PART = BANK // P
 PAIR_BLOCKS = H // (2 * P)
-GROUPS = ((0, 512, 4), (512, 512, 4), (1024, 512, 4), (1536, 512, 4), (2048, 256, 4))
+GROUPS = (
+    ((0, 1536, 1), (1536, 768, 2)),
+    ((0, 512, 4), (512, 512, 4), (1024, 512, 4), (1536, 512, 4), (2048, 256, 4)),
+)
 
 FLOPS = 2 * P * U * GATES * (I + H)
 
@@ -110,7 +113,7 @@ def tile_grouptorchgru_w_e_kernel(tc, inputs, hidden, w_ih_words, w_ih_scales, w
         words_i32 = w_ih_words.bitcast(I32)
 
         def load_words(u, group):
-            first_col, n_cols, n_passes = GROUPS[group]
+            first_col, n_cols, n_passes = GROUPS[u][group]
             tiles = []
             for first_pass in range(0, PASSES, n_passes):
                 tile_u8 = words_pool.tile(
@@ -134,7 +137,7 @@ def tile_grouptorchgru_w_e_kernel(tc, inputs, hidden, w_ih_words, w_ih_scales, w
             nc.sync.dma_start(out=x_sb[:, u, :], in_=inputs[:, u, :])
         for u in range(U):
             load_scales(u)
-        words = [[load_words(u, group) for group in range(len(GROUPS))] for u in range(U)]
+        words = [[load_words(u, group) for group in range(len(GROUPS[u]))] for u in range(U)]
 
         for u in range(U):
             h_bank = psum.tile([P, 2 * BANK], BF16, name="h_bank", tag="bank")
@@ -264,24 +267,26 @@ def tile_grouptorchgru_w_e_kernel(tc, inputs, hidden, w_ih_words, w_ih_scales, w
             )
 
         def multiply_group(u, group):
-            first_col, n_cols, n_passes = GROUPS[group]
-            width = min(n_cols, BANK) if n_cols >= BANK else NARROW
-            accs = [
-                psum.tile([P, BANK], F32, name="acc%d_%d" % (group, i), tag="bank") for i in range(n_cols // width)
-            ]
+            first_col, n_cols, n_passes = GROUPS[u][group]
+            starts = list(range(0, n_cols - n_cols % BANK, BANK)) + list(range(n_cols - n_cols % BANK, n_cols, NARROW))
+            pieces = []
+            for start in starts:
+                width = BANK if start + BANK <= n_cols else NARROW
+                acc = psum.tile([P, BANK], F32, name="acc%d_%d" % (group, start), tag="bank")
+                pieces.append((start, width, acc))
             for g in range(PASSES):
                 tile_u8 = words[u][group][g // n_passes]
-                for i in range(n_cols // width):
-                    start_byte = 2 * (n_cols * (g % n_passes) + width * i)
+                for start, width, acc in pieces:
+                    start_byte = 2 * (n_cols * (g % n_passes) + start)
                     mx_pass(
-                        accs[i][:, 0:width],
+                        acc[:, 0:width],
                         u,
                         g,
                         tile_u8[:, start_byte : start_byte + 2 * width],
-                        first_col + width * i,
+                        first_col + start,
                         width,
                     )
-            return accs
+            return pieces
 
         for u in range(U):
             gh_u = gh_sb[:, GATES * u : GATES * (u + 1)]
@@ -294,10 +299,13 @@ def tile_grouptorchgru_w_e_kernel(tc, inputs, hidden, w_ih_words, w_ih_scales, w
             old_part = gate_pool.tile([P, H], F32, name="old_part")
             result = gate_pool.tile([P, H], F32, name="result")
 
-            def add_hidden_part(group, acc):
-                cols = slice(BANK * group, BANK * (group + 1))
-                nc.vector.tensor_add(out=pre[:, cols], in0=acc[:], in1=gh_u[:, cols])
-                nc.scalar.activation(out=gates[:, cols], in_=pre[:, cols], func=SIGMOID)
+            def add_hidden_part(first_col, pieces):
+                for start, width, acc in pieces:
+                    cols = slice(first_col + start, first_col + start + width)
+                    nc.vector.tensor_add(out=pre[:, cols], in0=acc[:, 0:width], in1=gh_u[:, cols])
+
+            def sigmoid_part(lo, hi):
+                nc.scalar.activation(out=gates[:, lo:hi], in_=pre[:, lo:hi], func=SIGMOID)
 
             def keep_new_part(lo, hi):
                 nc.scalar.activation(out=keep_new[:, lo:hi], in_=pre[:, H + lo : H + hi], func=SIGMOID, scale=-1.0)
@@ -311,38 +319,64 @@ def tile_grouptorchgru_w_e_kernel(tc, inputs, hidden, w_ih_words, w_ih_scales, w
             def old_part_part(lo, hi):
                 nc.vector.tensor_mul(out=old_part[:, lo:hi], in0=gates[:, H + lo : H + hi], in1=hidden_sb[:, u, lo:hi])
 
-            split = 2 * BANK - H
-            accs = multiply_group(u, 0)
-            add_hidden_part(0, accs[0])
+            def add_new_part(first_col, pieces):
+                for start, width, acc in pieces:
+                    cols = slice(first_col + start, first_col + start + width)
+                    nc.vector.tensor_add(out=cand[:, cols], in0=acc[:, 0:width], in1=cand[:, cols])
 
-            accs = multiply_group(u, 1)
-            add_hidden_part(1, accs[0])
-            keep_new_part(0, split)
-            cand_part(0, BANK)
+            def tanh_part(lo, hi):
+                nc.scalar.activation(out=cand[:, lo:hi], in_=cand[:, lo:hi], func=TANH)
 
-            accs = multiply_group(u, 2)
-            add_hidden_part(2, accs[0])
-            keep_new_part(split, H)
-            cand_part(BANK, H)
-            cand_bias_part(0, BANK)
-            old_part_part(0, split)
-            cand_bias_part(BANK, H)
+            def blend_new_part(lo, hi):
+                nc.vector.tensor_mul(out=result[:, lo:hi], in0=cand[:, lo:hi], in1=keep_new[:, lo:hi])
 
-            head = slice(0, BANK)
-            tail = slice(BANK, H)
-            accs = multiply_group(u, 3)
-            nc.vector.tensor_add(out=cand[:, head], in0=accs[0][:], in1=cand[:, head])
-            nc.scalar.activation(out=cand[:, head], in_=cand[:, head], func=TANH)
-            old_part_part(split, H)
+            def finish_part(lo, hi):
+                nc.vector.tensor_add(out=result[:, lo:hi], in0=result[:, lo:hi], in1=old_part[:, lo:hi])
+                nc.sync.dma_start(out=out[:, u, lo:hi], in_=result[:, lo:hi])
 
-            accs = multiply_group(u, 4)
-            nc.vector.tensor_mul(out=result[:, head], in0=cand[:, head], in1=keep_new[:, head])
-            for i in range(2):
-                cols = slice(BANK + NARROW * i, BANK + NARROW * (i + 1))
-                nc.vector.tensor_add(out=cand[:, cols], in0=accs[i][:, 0:NARROW], in1=cand[:, cols])
-            nc.scalar.activation(out=cand[:, tail], in_=cand[:, tail], func=TANH)
-            nc.vector.tensor_add(out=result[:, head], in0=result[:, head], in1=old_part[:, head])
-            nc.sync.dma_start(out=out[:, u, head], in_=result[:, head])
-            nc.vector.tensor_mul(out=result[:, tail], in0=cand[:, tail], in1=keep_new[:, tail])
-            nc.vector.tensor_add(out=result[:, tail], in0=result[:, tail], in1=old_part[:, tail])
-            nc.sync.dma_start(out=out[:, u, tail], in_=result[:, tail])
+            if u == 0:
+                pieces = multiply_group(u, 0)
+                add_hidden_part(0, pieces)
+                sigmoid_part(0, H)
+                sigmoid_part(H, 2 * H)
+                keep_new_part(0, H)
+                pieces = multiply_group(u, 1)
+                cand_part(0, H)
+                old_part_part(0, H)
+                cand_bias_part(0, H)
+                add_new_part(0, pieces)
+                tanh_part(0, BANK)
+                tanh_part(BANK, H)
+                blend_new_part(0, BANK)
+                blend_new_part(BANK, H)
+                finish_part(0, BANK)
+                finish_part(BANK, H)
+            else:
+                split = 2 * BANK - H
+                add_hidden_part(0, multiply_group(u, 0))
+                sigmoid_part(0, BANK)
+
+                add_hidden_part(BANK, multiply_group(u, 1))
+                sigmoid_part(BANK, 2 * BANK)
+                keep_new_part(0, split)
+                cand_part(0, BANK)
+
+                add_hidden_part(2 * BANK, multiply_group(u, 2))
+                sigmoid_part(2 * BANK, 3 * BANK)
+                keep_new_part(split, H)
+                cand_part(BANK, H)
+                cand_bias_part(0, BANK)
+                old_part_part(0, split)
+                cand_bias_part(BANK, H)
+
+                add_new_part(0, multiply_group(u, 3))
+                tanh_part(0, BANK)
+                old_part_part(split, H)
+
+                pieces = multiply_group(u, 4)
+                blend_new_part(0, BANK)
+                add_new_part(BANK, pieces)
+                tanh_part(BANK, H)
+                finish_part(0, BANK)
+                blend_new_part(BANK, H)
+                finish_part(BANK, H)

@@ -31,6 +31,8 @@ GROUPS = (
     ((0, 512, 4), (512, 512, 4), (1024, 512, 4), (1536, 512, 4), (2048, 256, 4)),
 )
 
+X_AFTER_CHUNK = W_CHUNKS - 4
+
 FLOPS = 2 * P * U * GATES * (I + H)
 
 
@@ -59,7 +61,7 @@ def tile_grouptorchgru_w_e_kernel(tc, inputs, hidden, w_ih_words, w_ih_scales, w
         planes = []
         for u in range(U):
             plane = keep.tile([P, PASSES, GATES], U8, name="plane%d" % u, align_bytes=64)
-            nc.vector.memset(plane[:].bitcast(I32), 0)
+            nc.gpsimd.memset(plane[:].bitcast(F32), 0.0)
             planes.append(plane)
 
         warm = keep.tile([P, 1], F32)
@@ -131,10 +133,12 @@ def tile_grouptorchgru_w_e_kernel(tc, inputs, hidden, w_ih_words, w_ih_scales, w
             return tiles
 
         nc.sync.dma_start(out=hidden_sb[:], in_=hidden)
-        for c in range(W_CHUNKS):
+        for c in range(X_AFTER_CHUNK + 1):
             load_w_chunk(c)
         for u in range(U):
             nc.sync.dma_start(out=x_sb[:, u, :], in_=inputs[:, u, :])
+        for c in range(X_AFTER_CHUNK + 1, W_CHUNKS):
+            load_w_chunk(c)
         for u in range(U):
             load_scales(u)
         words = [[load_words(u, group) for group in range(len(GROUPS[u]))] for u in range(U)]
@@ -207,41 +211,37 @@ def tile_grouptorchgru_w_e_kernel(tc, inputs, hidden, w_ih_words, w_ih_scales, w
                 )
             nc.scalar.copy(out=gh_sb[:, BANK * c : BANK * (c + 1)], in_=acc[:])
 
-        for s in range(2 * PAIR_BLOCKS):
-            transpose_two(0, s)
-        for c in range(W_CHUNKS):
-            multiply_w_chunk(c)
+        staged = {}
 
-        def quantise_inputs(u):
+        def transpose_inputs(u, q):
             pairs = x_sb[:, u, :].bitcast(F32)
-            staged = []
-            for q in range(2):
-                grouped = grouped_pool.tile([P, 4 * K_PASS], BF16, name="grouped", tag="grouped", align_bytes=64)
-                grouped_pairs = grouped[:].bitcast(F32)
-                for h in range(2):
-                    bank = psum.tile([P, BANK], F32, name="x_bank", tag="bank")
-                    for g2 in range(2):
-                        g = 4 * q + 2 * h + g2
-                        for w in range(2):
-                            nc.tensor.transpose(
-                                bank[:, P * (2 * g2 + w) : P * (2 * g2 + w + 1)],
-                                pairs[:, 2 * P * g + w : 2 * P * (g + 1) : 2],
-                                ident_f32[:],
-                            )
-                    dst = grouped_pairs[:, BANK * h : BANK * (h + 1)].rearrange("p (g b w) -> p g b w", g=2, w=2)
-                    src = bank[:].rearrange("p (g w b) -> p g b w", g=2, w=2)
-                    if h == 0:
-                        nc.scalar.copy(out=dst, in_=src)
-                    else:
-                        nc.vector.tensor_copy(out=dst, in_=src)
-                staged.append(grouped)
-            for q in range(2):
-                four = slice(PASSES * u + 4 * q, PASSES * u + 4 * q + 4)
-                nc.vector.quantize_mx(
-                    out=x_codes[:, four, :].rearrange("p g b -> p (g b)").bitcast(FP8X4),
-                    scales=x_scales[:, four, :].rearrange("p g b -> p (g b)"),
-                    in_=staged[q][:],
-                )
+            grouped = grouped_pool.tile([P, 4 * K_PASS], BF16, name="grouped", tag="grouped", align_bytes=64)
+            grouped_pairs = grouped[:].bitcast(F32)
+            for h in range(2):
+                bank = psum.tile([P, BANK], F32, name="x_bank", tag="bank")
+                for g2 in range(2):
+                    g = 4 * q + 2 * h + g2
+                    for w in range(2):
+                        nc.tensor.transpose(
+                            bank[:, P * (2 * g2 + w) : P * (2 * g2 + w + 1)],
+                            pairs[:, 2 * P * g + w : 2 * P * (g + 1) : 2],
+                            ident_f32[:],
+                        )
+                dst = grouped_pairs[:, BANK * h : BANK * (h + 1)].rearrange("p (g b w) -> p g b w", g=2, w=2)
+                src = bank[:].rearrange("p (g w b) -> p g b w", g=2, w=2)
+                if h == 0:
+                    nc.scalar.copy(out=dst, in_=src)
+                else:
+                    nc.vector.tensor_copy(out=dst, in_=src)
+            staged[(u, q)] = grouped
+
+        def quantise_inputs(u, q):
+            four = slice(PASSES * u + 4 * q, PASSES * u + 4 * q + 4)
+            nc.vector.quantize_mx(
+                out=x_codes[:, four, :].rearrange("p g b -> p (g b)").bitcast(FP8X4),
+                scales=x_scales[:, four, :].rearrange("p g b -> p (g b)"),
+                in_=staged[(u, q)][:],
+            )
 
         def spread_new_bias():
             for i in range(U * H // BANK):
@@ -251,9 +251,17 @@ def tile_grouptorchgru_w_e_kernel(tc, inputs, hidden, w_ih_words, w_ih_scales, w
                 )
                 nc.scalar.copy(out=bias_new_sb[:, BANK * i : BANK * (i + 1)], in_=acc[:])
 
-        quantise_inputs(0)
+        for s in range(2 * PAIR_BLOCKS):
+            transpose_two(0, s)
         spread_new_bias()
-        quantise_inputs(1)
+        for c in range(W_CHUNKS):
+            multiply_w_chunk(c)
+            step = c - X_AFTER_CHUNK
+            if step >= 0:
+                transpose_inputs(step // 2, step % 2)
+            if step >= 1:
+                quantise_inputs((step - 1) // 2, (step - 1) % 2)
+        quantise_inputs(U - 1, 1)
 
         def mx_pass(acc, u, g, words, first_col, width):
             nc.tensor.matmul_mx(

@@ -27,8 +27,8 @@ W_CHUNKS = U * GATES // BANK
 ROWS_PER_PART = BANK // P
 PAIR_BLOCKS = H // (2 * P)
 GROUPS = (
-    ((0, 1536, 1), (1536, 768, 2)),
-    ((0, 512, 4), (512, 512, 4), (1024, 512, 4), (1536, 512, 4), (2048, 256, 4)),
+    ((0, 1536, (1,) * 8), (1536, 768, (2,) * 4)),
+    ((0, 1024, (2,) * 4), (1024, 512, (4, 4)), (1536, 512, (4, 4)), (2048, 256, (4, 3, 1))),
 )
 
 X_AFTER_CHUNK = W_CHUNKS - 4
@@ -115,9 +115,10 @@ def tile_grouptorchgru_w_e_kernel(tc, inputs, hidden, w_ih_words, w_ih_scales, w
         words_i32 = w_ih_words.bitcast(I32)
 
         def load_words(u, group):
-            first_col, n_cols, n_passes = GROUPS[u][group]
-            tiles = []
-            for first_pass in range(0, PASSES, n_passes):
+            first_col, n_cols, loads = GROUPS[u][group]
+            by_pass = []
+            for n_passes in loads:
+                first_pass = len(by_pass)
                 tile_u8 = words_pool.tile(
                     [P, n_passes * n_cols * 2], U8, name="w%d_%d_%d" % (u, group, first_pass), tag="words", align_bytes=64
                 )
@@ -129,8 +130,8 @@ def tile_grouptorchgru_w_e_kernel(tc, inputs, hidden, w_ih_words, w_ih_scales, w
                         first_col // 2 : (first_col + n_cols) // 2,
                     ].rearrange("g p c -> p g c"),
                 )
-                tiles.append(tile_u8)
-            return tiles
+                by_pass.extend([(tile_u8, i) for i in range(n_passes)])
+            return by_pass
 
         nc.sync.dma_start(out=hidden_sb[:], in_=hidden)
         for c in range(X_AFTER_CHUNK + 1):
@@ -275,7 +276,7 @@ def tile_grouptorchgru_w_e_kernel(tc, inputs, hidden, w_ih_words, w_ih_scales, w
             )
 
         def multiply_group(u, group):
-            first_col, n_cols, n_passes = GROUPS[u][group]
+            first_col, n_cols = GROUPS[u][group][0:2]
             starts = list(range(0, n_cols - n_cols % BANK, BANK)) + list(range(n_cols - n_cols % BANK, n_cols, NARROW))
             pieces = []
             for start in starts:
@@ -283,9 +284,9 @@ def tile_grouptorchgru_w_e_kernel(tc, inputs, hidden, w_ih_words, w_ih_scales, w
                 acc = psum.tile([P, BANK], F32, name="acc%d_%d" % (group, start), tag="bank")
                 pieces.append((start, width, acc))
             for g in range(PASSES):
-                tile_u8 = words[u][group][g // n_passes]
+                tile_u8, place = words[u][group][g]
                 for start, width, acc in pieces:
-                    start_byte = 2 * (n_cols * (g % n_passes) + start)
+                    start_byte = 2 * (n_cols * place + start)
                     mx_pass(
                         acc[:, 0:width],
                         u,
@@ -363,25 +364,23 @@ def tile_grouptorchgru_w_e_kernel(tc, inputs, hidden, w_ih_words, w_ih_scales, w
                 split = 2 * BANK - H
                 add_hidden_part(0, multiply_group(u, 0))
                 sigmoid_part(0, BANK)
-
-                add_hidden_part(BANK, multiply_group(u, 1))
                 sigmoid_part(BANK, 2 * BANK)
                 keep_new_part(0, split)
                 cand_part(0, BANK)
-
-                add_hidden_part(2 * BANK, multiply_group(u, 2))
-                sigmoid_part(2 * BANK, 3 * BANK)
-                keep_new_part(split, H)
                 cand_part(BANK, H)
                 cand_bias_part(0, BANK)
-                old_part_part(0, split)
                 cand_bias_part(BANK, H)
+                old_part_part(0, split)
 
-                add_new_part(0, multiply_group(u, 3))
+                add_hidden_part(2 * BANK, multiply_group(u, 1))
+                sigmoid_part(2 * BANK, 3 * BANK)
+                keep_new_part(split, H)
+
+                add_new_part(0, multiply_group(u, 2))
                 tanh_part(0, BANK)
                 old_part_part(split, H)
 
-                pieces = multiply_group(u, 4)
+                pieces = multiply_group(u, 3)
                 blend_new_part(0, BANK)
                 add_new_part(BANK, pieces)
                 tanh_part(BANK, H)

@@ -90,9 +90,9 @@ def tile_grouptorchgru_w_e_kernel(tc, inputs, hidden, w_ih_words, w_ih_scales, w
         w_flat = w_hh.flatten_outer_dims()
         w_rows = []
 
-        def load_w_chunk(c):
+        def load_w_chunk(c, queue):
             rows = w_rows_pool.tile([P, ROWS_PER_PART, H], BF16, name="rows%d" % c, tag="rows")
-            nc.sync.dma_start(
+            queue.dma_start(
                 out=rows[:],
                 in_=w_flat[BANK * c : BANK * (c + 1), :].rearrange("(p j) k -> p j k", j=ROWS_PER_PART),
             )
@@ -135,11 +135,11 @@ def tile_grouptorchgru_w_e_kernel(tc, inputs, hidden, w_ih_words, w_ih_scales, w
 
         nc.sync.dma_start(out=hidden_sb[:], in_=hidden)
         for c in range(X_AFTER_CHUNK + 1):
-            load_w_chunk(c)
+            load_w_chunk(c, nc.scalar if c % 2 == 1 else nc.sync)
         for u in range(U):
             nc.sync.dma_start(out=x_sb[:, u, :], in_=inputs[:, u, :])
         for c in range(X_AFTER_CHUNK + 1, W_CHUNKS):
-            load_w_chunk(c)
+            load_w_chunk(c, nc.sync)
         for u in range(U):
             load_scales(u)
         words = [[load_words(u, group) for group in range(len(GROUPS[u]))] for u in range(U)]
@@ -380,10 +380,9 @@ def tile_grouptorchgru_w_e_kernel(tc, inputs, hidden, w_ih_words, w_ih_scales, w
                 tanh_part(0, BANK)
                 old_part_part(split, H)
 
-                pieces = multiply_group(u, 3)
-                blend_new_part(0, BANK)
-                add_new_part(BANK, pieces)
+                add_new_part(BANK, multiply_group(u, 3))
                 tanh_part(BANK, H)
+                blend_new_part(0, BANK)
                 finish_part(0, BANK)
                 blend_new_part(BANK, H)
                 finish_part(BANK, H)

@@ -28,7 +28,7 @@ ROWS_PER_PART = BANK // P
 PAIR_BLOCKS = H // (2 * P)
 GROUPS = (
     ((0, 1536, (1,) * 8), (1536, 768, (2,) * 4)),
-    ((0, 1024, (2,) * 4), (1024, 512, (4, 4)), (1536, 512, (4, 4)), (2048, 256, (4, 3, 1))),
+    ((0, 1024, (2,) * 4), (1024, 512, (2,) * 4), (1536, 512, (2, 2, 2, 1, 1)), (2048, 256, (2, 2, 2, 1, 1))),
 )
 
 X_AFTER_CHUNK = W_CHUNKS - 4

@@ -33,6 +33,8 @@ GROUPS = (
 
 X_AFTER_CHUNK = W_CHUNKS - 4
 
+WARM_STEPS = 3
+
 FLOPS = 2 * P * U * GATES * (I + H)
 
 
@@ -66,6 +68,12 @@ def tile_grouptorchgru_w_e_kernel(tc, inputs, hidden, w_ih_words, w_ih_scales, w
 
         warm = keep.tile([P, 1], F32)
         nc.scalar.activation(out=warm[:], in_=ones[:, 0:1], func=SIGMOID)
+
+        late_ones = []
+        for i in range(WARM_STEPS):
+            late = keep.tile([P, P], BF16, name="late_ones%d" % i)
+            late_ones.append(late)
+        probe = keep.tile([P, WARM_STEPS * 16], I32)
 
         hidden_sb = keep.tile([P, U, H], BF16)
         hidden_t = keep.tile([P, U, 2 * PAIR_BLOCKS, P], BF16)
@@ -244,17 +252,31 @@ def tile_grouptorchgru_w_e_kernel(tc, inputs, hidden, w_ih_words, w_ih_scales, w
                 in_=staged[(u, q)][:],
             )
 
-        def spread_new_bias():
+        def spread_new_bias(all_ones):
             for i in range(U * H // BANK):
                 acc = psum.tile([P, BANK], F32, name="bias_bank", tag="bank")
                 nc.tensor.matmul(
-                    out=acc[:], lhsT=ones[:], rhs=bias_new_rows[:, BANK * i : BANK * (i + 1)], start=True, stop=True
+                    out=acc[:], lhsT=all_ones, rhs=bias_new_rows[:, BANK * i : BANK * (i + 1)], start=True, stop=True
                 )
                 nc.scalar.copy(out=bias_new_sb[:, BANK * i : BANK * (i + 1)], in_=acc[:])
 
+        def idle_matmuls(all_ones, count):
+            acc = psum.tile([P, BANK], F32, name="idle_bank", tag="bank")
+            for i in range(count):
+                nc.tensor.matmul(out=acc[:], lhsT=all_ones, rhs=bias_rows[:, 0:BANK], start=True, stop=True)
+
+        def warm_up():
+            late_bytes = (planes[1][:, 0, 0:64], planes[1][0:32, 4, 0:64], planes[1][32:64, 4, 0:64])
+            probes = (probe[:, 0:16], probe[0:32, 16:32], probe[32:64, 32:48])
+            for i in range(WARM_STEPS):
+                nc.gpsimd.tensor_copy(out=probes[i], in_=late_bytes[i].bitcast(I32))
+                nc.gpsimd.tensor_copy(out=late_ones[i][:], in_=ones[:])
+            idle_matmuls(late_ones[0][:], 3)
+            spread_new_bias(late_ones[1][:])
+            idle_matmuls(late_ones[2][:], 2)
+
         for s in range(2 * PAIR_BLOCKS):
             transpose_two(0, s)
-        spread_new_bias()
         for c in range(W_CHUNKS):
             multiply_w_chunk(c)
             step = c - X_AFTER_CHUNK
@@ -263,6 +285,7 @@ def tile_grouptorchgru_w_e_kernel(tc, inputs, hidden, w_ih_words, w_ih_scales, w
             if step >= 1:
                 quantise_inputs((step - 1) // 2, (step - 1) % 2)
         quantise_inputs(U - 1, 1)
+        warm_up()
 
         def mx_pass(acc, u, g, words, first_col, width):
             nc.tensor.matmul_mx(

@@ -42,10 +42,9 @@ def tile_grouptorchgru_w_e_kernel(tc, inputs, hidden, w_ih_words, w_ih_scales, w
     nc = tc.nc
     with ExitStack() as ctx:
         keep = ctx.enter_context(tc.tile_pool(name="keep", bufs=1))
-        w_rows_pool = ctx.enter_context(tc.tile_pool(name="w_rows", bufs=6))
+        stream_pool = ctx.enter_context(tc.tile_pool(name="stream", bufs=12))
         w_cols_pool = ctx.enter_context(tc.tile_pool(name="w_cols", bufs=3))
         grouped_pool = ctx.enter_context(tc.tile_pool(name="grouped", bufs=2))
-        words_pool = ctx.enter_context(tc.tile_pool(name="words", bufs=9))
         gate_pool = ctx.enter_context(tc.tile_pool(name="gate", bufs=1))
         psum = ctx.enter_context(tc.psum_pool(name="psum", bufs=8))
 
@@ -96,15 +95,15 @@ def tile_grouptorchgru_w_e_kernel(tc, inputs, hidden, w_ih_words, w_ih_scales, w
         )
 
         w_flat = w_hh.flatten_outer_dims()
-        w_rows = []
+        w_rows = {}
 
         def load_w_chunk(c, queue):
-            rows = w_rows_pool.tile([P, ROWS_PER_PART, H], BF16, name="rows%d" % c, tag="rows")
+            rows = stream_pool.tile([P, ROWS_PER_PART, H], BF16, name="rows%d" % c, tag="stream", align_bytes=64)
             queue.dma_start(
                 out=rows[:],
                 in_=w_flat[BANK * c : BANK * (c + 1), :].rearrange("(p j) k -> p j k", j=ROWS_PER_PART),
             )
-            w_rows.append(rows)
+            w_rows[c] = rows
 
         scale_rows = w_ih_scales.bitcast(I32).rearrange("g q c -> q g c")
 
@@ -127,8 +126,8 @@ def tile_grouptorchgru_w_e_kernel(tc, inputs, hidden, w_ih_words, w_ih_scales, w
             by_pass = []
             for n_passes in loads:
                 first_pass = len(by_pass)
-                tile_u8 = words_pool.tile(
-                    [P, n_passes * n_cols * 2], U8, name="w%d_%d_%d" % (u, group, first_pass), tag="words", align_bytes=64
+                tile_u8 = stream_pool.tile(
+                    [P, n_passes * n_cols * 2], U8, name="w%d_%d_%d" % (u, group, first_pass), tag="stream", align_bytes=64
                 )
                 nc.sync.dma_start(
                     out=tile_u8[:].bitcast(I32).rearrange("p (g c) -> p g c", g=n_passes),
@@ -144,13 +143,17 @@ def tile_grouptorchgru_w_e_kernel(tc, inputs, hidden, w_ih_words, w_ih_scales, w
         nc.sync.dma_start(out=hidden_sb[:], in_=hidden)
         for c in range(X_AFTER_CHUNK + 1):
             load_w_chunk(c, nc.scalar if c % 2 == 1 else nc.sync)
-        for u in range(U):
-            nc.sync.dma_start(out=x_sb[:, u, :], in_=inputs[:, u, :])
-        for c in range(X_AFTER_CHUNK + 1, W_CHUNKS):
-            load_w_chunk(c, nc.sync)
-        for u in range(U):
-            load_scales(u)
-        words = [[load_words(u, group) for group in range(len(GROUPS[u]))] for u in range(U)]
+        nc.sync.dma_start(out=x_sb[:, 0, :], in_=inputs[:, 0, :])
+        nc.scalar.dma_start(out=x_sb[:, 1, :], in_=inputs[:, 1, :])
+        load_w_chunk(6, nc.sync)
+        load_w_chunk(8, nc.sync)
+        words = []
+
+        def load_the_rest():
+            load_w_chunk(7, nc.scalar)
+            for u in range(U):
+                load_scales(u)
+            words.extend([[load_words(u, group) for group in range(len(GROUPS[u]))] for u in range(U)])
 
         for u in range(U):
             h_bank = psum.tile([P, 2 * BANK], BF16, name="h_bank", tag="bank")
@@ -279,6 +282,8 @@ def tile_grouptorchgru_w_e_kernel(tc, inputs, hidden, w_ih_words, w_ih_scales, w
             transpose_two(0, s)
         for c in range(W_CHUNKS):
             multiply_w_chunk(c)
+            if c == 0:
+                load_the_rest()
             step = c - X_AFTER_CHUNK
             if step >= 0:
                 transpose_inputs(step // 2, step % 2)

@@ -27,8 +27,13 @@ W_CHUNKS = U * GATES // BANK
 ROWS_PER_PART = BANK // P
 PAIR_BLOCKS = H // (2 * P)
 GROUPS = (
-    ((0, 1536, (1,) * 8), (1536, 768, (2,) * 4)),
-    ((0, 1024, (2,) * 4), (1024, 512, (2,) * 4), (1536, 512, (2, 2, 2, 1, 1)), (2048, 256, (2, 2, 2, 1, 1))),
+    ((0, 1536, ((1, 1),) * 4), (1536, 768, ((2, 2),) * 2)),
+    (
+        (0, 1024, ((2, 1), (2, 1), (2,))),
+        (1024, 512, ((2, 2, 2), (2,))),
+        (1536, 512, ((2, 2, 2), (1, 1))),
+        (2048, 256, ((2, 2, 2, 1, 1),)),
+    ),
 )
 
 X_AFTER_CHUNK = W_CHUNKS - 4
@@ -122,22 +127,26 @@ def tile_grouptorchgru_w_e_kernel(tc, inputs, hidden, w_ih_words, w_ih_scales, w
         words_i32 = w_ih_words.bitcast(I32)
 
         def load_words(u, group):
-            first_col, n_cols, loads = GROUPS[u][group]
+            first_col, n_cols, tiles = GROUPS[u][group]
             by_pass = []
-            for n_passes in loads:
-                first_pass = len(by_pass)
+            for loads in tiles:
                 tile_u8 = stream_pool.tile(
-                    [P, n_passes * n_cols * 2], U8, name="w%d_%d_%d" % (u, group, first_pass), tag="stream", align_bytes=64
+                    [P, sum(loads) * n_cols * 2], U8, name="w%d_%d_%d" % (u, group, len(by_pass)), tag="stream", align_bytes=64
                 )
-                nc.sync.dma_start(
-                    out=tile_u8[:].bitcast(I32).rearrange("p (g c) -> p g c", g=n_passes),
-                    in_=words_i32[
-                        PASSES * u + first_pass : PASSES * u + first_pass + n_passes,
-                        :,
-                        first_col // 2 : (first_col + n_cols) // 2,
-                    ].rearrange("g p c -> p g c"),
-                )
-                by_pass.extend([(tile_u8, i) for i in range(n_passes)])
+                by_word = tile_u8[:].bitcast(I32).rearrange("p (g c) -> p g c", g=sum(loads))
+                place = 0
+                for n_passes in loads:
+                    first_pass = len(by_pass)
+                    nc.sync.dma_start(
+                        out=by_word[:, place : place + n_passes, :],
+                        in_=words_i32[
+                            PASSES * u + first_pass : PASSES * u + first_pass + n_passes,
+                            :,
+                            first_col // 2 : (first_col + n_cols) // 2,
+                        ].rearrange("g p c -> p g c"),
+                    )
+                    by_pass.extend([(tile_u8, place + i) for i in range(n_passes)])
+                    place += n_passes
             return by_pass
 
         nc.sync.dma_start(out=hidden_sb[:], in_=hidden)

@@ -153,7 +153,6 @@ def tile_grouptorchgru_w_e_kernel(tc, inputs, hidden, w_ih_words, w_ih_scales, w
         for c in range(X_AFTER_CHUNK + 1):
             load_w_chunk(c, nc.scalar if c % 2 == 1 else nc.sync)
         nc.sync.dma_start(out=x_sb[:, 0, :], in_=inputs[:, 0, :])
-        nc.scalar.dma_start(out=x_sb[:, 1, :], in_=inputs[:, 1, :])
         load_w_chunk(6, nc.sync)
         load_w_chunk(8, nc.sync)
         words = []
@@ -176,6 +175,8 @@ def tile_grouptorchgru_w_e_kernel(tc, inputs, hidden, w_ih_words, w_ih_scales, w
             nc.scalar.copy(
                 out=hidden_t[:, u, :, :].rearrange("p s b -> p (s b)"), in_=h_bank[:, 0 : 2 * PAIR_BLOCKS * P]
             )
+
+        nc.scalar.dma_start(out=x_sb[:, 1, :], in_=inputs[:, 1, :])
 
         w_cols = []
         w_banks = []
@@ -383,16 +384,18 @@ def tile_grouptorchgru_w_e_kernel(tc, inputs, hidden, w_ih_words, w_ih_scales, w
             if u == 0:
                 pieces = multiply_group(u, 0)
                 add_hidden_part(0, pieces)
-                sigmoid_part(0, H)
-                sigmoid_part(H, 2 * H)
+                sigmoid_part(0, BANK)
+                sigmoid_part(BANK, 2 * BANK)
+                sigmoid_part(2 * BANK, 3 * BANK)
                 keep_new_part(0, H)
                 pieces = multiply_group(u, 1)
-                cand_part(0, H)
-                old_part_part(0, H)
+                cand_part(0, BANK)
+                cand_part(BANK, H)
                 cand_bias_part(0, H)
                 add_new_part(0, pieces)
                 tanh_part(0, BANK)
                 tanh_part(BANK, H)
+                old_part_part(0, H)
                 blend_new_part(0, BANK)
                 blend_new_part(BANK, H)
                 finish_part(0, BANK)
@@ -405,13 +408,12 @@ def tile_grouptorchgru_w_e_kernel(tc, inputs, hidden, w_ih_words, w_ih_scales, w
                 keep_new_part(0, split)
                 cand_part(0, BANK)
                 cand_part(BANK, H)
-                cand_bias_part(0, BANK)
-                cand_bias_part(BANK, H)
-                old_part_part(0, split)
 
                 add_hidden_part(2 * BANK, multiply_group(u, 1))
                 sigmoid_part(2 * BANK, 3 * BANK)
                 keep_new_part(split, H)
+                cand_bias_part(0, H)
+                old_part_part(0, split)
 
                 add_new_part(0, multiply_group(u, 2))
                 tanh_part(0, BANK)

from contextlib import ExitStack

import concourse.mybir as mybir
from concourse.masks import make_identity

F32 = mybir.dt.float32
BF16 = mybir.dt.bfloat16
I32 = mybir.dt.int32
U8 = mybir.dt.uint8
U32 = mybir.dt.uint32
FP8X4 = mybir.dt.float8_e4m3fn_x4
FP4X4 = mybir.dt.float4_e2m1fn_x4
SIGMOID = mybir.ActivationFunctionType.Sigmoid
TANH = mybir.ActivationFunctionType.Tanh

P = 128
U = 2
I = 4096
H = 768
GATES = 3 * H
K_PASS = 512
PASSES = I // K_PASS
BANK = 512
NARROW = 128

W_CHUNKS = U * GATES // BANK
ROWS_PER_PART = BANK // P
PAIR_BLOCKS = H // (2 * P)
GROUPS = (
    ((0, 1536, ((1, 1),) * 4), (1536, 768, ((2, 2),) * 2)),
    (
        (0, 1024, ((2, 1), (2, 1), (2,))),
        (1024, 512, ((2, 2, 2), (2,))),
        (1536, 512, ((2, 2, 2), (1, 1))),
        (2048, 256, ((2, 2, 2, 1, 1),)),
    ),
)

X_AFTER_CHUNK = W_CHUNKS - 4

WARM_STEPS = 3

FLOPS = 2 * P * U * GATES * (I + H)


def tile_grouptorchgru_w_e_kernel(tc, inputs, hidden, w_ih_words, w_ih_scales, w_hh, b_ih, b_hh, out):
    nc = tc.nc
    with ExitStack() as ctx:
        keep = ctx.enter_context(tc.tile_pool(name="keep", bufs=1))
        stream_pool = ctx.enter_context(tc.tile_pool(name="stream", bufs=12))
        w_cols_pool = ctx.enter_context(tc.tile_pool(name="w_cols", bufs=3))
        grouped_pool = ctx.enter_context(tc.tile_pool(name="grouped", bufs=2))
        gate_pool = ctx.enter_context(tc.tile_pool(name="gate", bufs=1))
        psum = ctx.enter_context(tc.psum_pool(name="psum", bufs=8))

        ident_f32 = keep.tile([P, P], F32)
        make_identity(nc, ident_f32[:])
        ident_bf16 = keep.tile([P, P], BF16)
        make_identity(nc, ident_bf16[:])

        ones = keep.tile([P, P], BF16)
        nc.vector.memset(ones[:], 1.0)
        bias_rows = keep.tile([P, U * GATES], BF16)
        nc.vector.memset(bias_rows[:].bitcast(I32), 0)
        bias_new_rows = keep.tile([P, U * H], BF16)
        nc.vector.memset(bias_new_rows[:].bitcast(I32), 0)
        planes = []
        for u in range(U):
            plane = keep.tile([P, PASSES, GATES], U8, name="plane%d" % u, align_bytes=64)
            nc.gpsimd.memset(plane[:].bitcast(F32), 0.0)
            planes.append(plane)

        warm = keep.tile([P, 1], F32)
        nc.scalar.activation(out=warm[:], in_=ones[:, 0:1], func=SIGMOID)

        late_ones = []
        for i in range(WARM_STEPS):
            late = keep.tile([P, P], BF16, name="late_ones%d" % i)
            late_ones.append(late)
        probe = keep.tile([P, WARM_STEPS * 16], I32)

        hidden_sb = keep.tile([P, U, H], BF16)
        hidden_t = keep.tile([P, U, 2 * PAIR_BLOCKS, P], BF16)
        gh_sb = keep.tile([P, U * GATES], F32)
        bias_new_sb = keep.tile([P, U * H], F32)
        x_sb = keep.tile([P, U, I], BF16)
        x_codes = keep.tile([P, U * PASSES, P], U32, align_bytes=64)
        x_scales = keep.tile([P, U * PASSES, P], U8, align_bytes=64)

        ctx.enter_context(tc.manual_schedule())

        nc.scalar.dma_start(out=bias_rows[0:1, :], in_=b_hh.rearrange("u n -> (u n)").unsqueeze(0))
        nc.scalar.dma_start(
            out=bias_rows[1:2, :].rearrange("o (u n) -> o u n", u=U)[:, :, 0 : 2 * H],
            in_=b_ih.unsqueeze(0)[:, :, 0 : 2 * H],
        )
        nc.scalar.dma_start(
            out=bias_new_rows[0:1, :].rearrange("o (u n) -> o u n", u=U),
            in_=b_ih.unsqueeze(0)[:, :, 2 * H : 3 * H],
        )

        w_flat = w_hh.flatten_outer_dims()
        w_rows = {}

        def load_w_chunk(c, queue):
            rows = stream_pool.tile([P, ROWS_PER_PART, H], BF16, name="rows%d" % c, tag="stream", align_bytes=64)
            queue.dma_start(
                out=rows[:],
                in_=w_flat[BANK * c : BANK * (c + 1), :].rearrange("(p j) k -> p j k", j=ROWS_PER_PART),
            )
            w_rows[c] = rows

        scale_rows = w_ih_scales.bitcast(I32).rearrange("g q c -> q g c")

        def load_scales(u):
            plane = planes[u][:].bitcast(I32)
            for half in range(2):
                local = slice(4 * half, 4 * half + 4)
                given = slice(PASSES * u + 4 * half, PASSES * u + 4 * half + 4)
                for b in range(2):
                    for r in range(4):
                        nc.sync.dma_start(
                            out=plane[32 * b + r : P : 64, local, :],
                            in_=scale_rows[4 * b + r : 16 : 8, given, :],
                        )

        words_i32 = w_ih_words.bitcast(I32)

        def load_words(u, group):
            first_col, n_cols, tiles = GROUPS[u][group]
            by_pass = []
            for loads in tiles:
                tile_u8 = stream_pool.tile(
                    [P, sum(loads) * n_cols * 2], U8, name="w%d_%d_%d" % (u, group, len(by_pass)), tag="stream", align_bytes=64
                )
                by_word = tile_u8[:].bitcast(I32).rearrange("p (g c) -> p g c", g=sum(loads))
                place = 0
                for n_passes in loads:
                    first_pass = len(by_pass)
                    nc.sync.dma_start(
                        out=by_word[:, place : place + n_passes, :],
                        in_=words_i32[
                            PASSES * u + first_pass : PASSES * u + first_pass + n_passes,
                            :,
                            first_col // 2 : (first_col + n_cols) // 2,
                        ].rearrange("g p c -> p g c"),
                    )
                    by_pass.extend([(tile_u8, place + i) for i in range(n_passes)])
                    place += n_passes
            return by_pass

        nc.sync.dma_start(out=hidden_sb[:], in_=hidden)
        for c in range(X_AFTER_CHUNK + 1):
            load_w_chunk(c, nc.scalar if c % 2 == 1 else nc.sync)
        nc.sync.dma_start(out=x_sb[:, 0, :], in_=inputs[:, 0, :])
        load_w_chunk(6, nc.sync)
        load_w_chunk(8, nc.sync)
        words = []

        def load_the_rest():
            load_w_chunk(7, nc.scalar)
            for u in range(U):
                load_scales(u)
            words.extend([[load_words(u, group) for group in range(len(GROUPS[u]))] for u in range(U)])

        for u in range(U):
            h_bank = psum.tile([P, 2 * BANK], BF16, name="h_bank", tag="bank")
            for s in range(2 * PAIR_BLOCKS):
                kb, e = divmod(s, 2)
                nc.tensor.transpose(
                    h_bank[:, P * s : P * (s + 1)],
                    hidden_sb[:, u, 2 * P * kb + e : 2 * P * (kb + 1) : 2],
                    ident_bf16[:],
                )
            nc.scalar.copy(
                out=hidden_t[:, u, :, :].rearrange("p s b -> p (s b)"), in_=h_bank[:, 0 : 2 * PAIR_BLOCKS * P]
            )

        nc.scalar.dma_start(out=x_sb[:, 1, :], in_=inputs[:, 1, :])

        w_cols = []
        w_banks = []

        def transpose_two(c, s):
            kb, half = divmod(s, 2)
            if s == 0:
                w_cols.append(w_cols_pool.tile([P, PAIR_BLOCKS, BANK], F32, name="cols%d" % c, tag="cols"))
                w_banks.append([])
            if half == 0:
                w_banks[c].append(psum.tile([P, BANK], F32, name="w_bank", tag="bank"))
            bank = w_banks[c][kb]
            pairs = w_rows[c][:].bitcast(F32)
            for j in (2 * half, 2 * half + 1):
                nc.tensor.transpose(bank[:, P * j : P * (j + 1)], pairs[:, j, P * kb : P * (kb + 1)], ident_f32[:])
            if half == 1:
                dst = w_cols[c][:, kb, :].rearrange("p (r j) -> p r j", j=ROWS_PER_PART)
                src = bank[:].rearrange("p (j r) -> p r j", j=ROWS_PER_PART)
                if kb == 1:
                    nc.scalar.copy(out=dst, in_=src)
                else:
                    nc.vector.tensor_copy(out=dst, in_=src)

        def units_in_chunk(c):
            pieces = []
            for u in range(U):
                lo = max(BANK * c, GATES * u)
                hi = min(BANK * (c + 1), GATES * (u + 1))
                if lo < hi:
                    pieces.append((u, lo - BANK * c, hi - BANK * c))
            return pieces

        def multiply_w_chunk(c):
            halves = w_cols[c][:].bitcast(BF16).rearrange("p k (n e) -> p k n e", e=2)
            acc = psum.tile([P, BANK], F32, name="gh_bank", tag="bank")
            for piece, (u, lo, hi) in enumerate(units_in_chunk(c)):
                for s in range(2 * PAIR_BLOCKS):
                    kb, e = divmod(s, 2)
                    nc.tensor.matmul(
                        out=acc[:, lo:hi],
                        lhsT=hidden_t[:, u, s, :],
                        rhs=halves[:, kb, lo:hi, e],
                        start=(s == 0),
                        stop=False,
                    )
                    if piece == 0 and c + 1 < W_CHUNKS:
                        transpose_two(c + 1, s)
                nc.tensor.matmul(
                    out=acc[:, lo:hi],
                    lhsT=ones[:],
                    rhs=bias_rows[:, BANK * c + lo : BANK * c + hi],
                    start=False,
                    stop=True,
                )
            nc.scalar.copy(out=gh_sb[:, BANK * c : BANK * (c + 1)], in_=acc[:])

        staged = {}

        def transpose_inputs(u, q):
            pairs = x_sb[:, u, :].bitcast(F32)
            grouped = grouped_pool.tile([P, 4 * K_PASS], BF16, name="grouped", tag="grouped", align_bytes=64)
            grouped_pairs = grouped[:].bitcast(F32)
            for h in range(2):
                bank = psum.tile([P, BANK], F32, name="x_bank", tag="bank")
                for g2 in range(2):
                    g = 4 * q + 2 * h + g2
                    for w in range(2):
                        nc.tensor.transpose(
                            bank[:, P * (2 * g2 + w) : P * (2 * g2 + w + 1)],
                            pairs[:, 2 * P * g + w : 2 * P * (g + 1) : 2],
                            ident_f32[:],
                        )
                dst = grouped_pairs[:, BANK * h : BANK * (h + 1)].rearrange("p (g b w) -> p g b w", g=2, w=2)
                src = bank[:].rearrange("p (g w b) -> p g b w", g=2, w=2)
                if h == 0:
                    nc.scalar.copy(out=dst, in_=src)
                else:
                    nc.vector.tensor_copy(out=dst, in_=src)
            staged[(u, q)] = grouped

        def quantise_inputs(u, q):
            four = slice(PASSES * u + 4 * q, PASSES * u + 4 * q + 4)
            nc.vector.quantize_mx(
                out=x_codes[:, four, :].rearrange("p g b -> p (g b)").bitcast(FP8X4),
                scales=x_scales[:, four, :].rearrange("p g b -> p (g b)"),
                in_=staged[(u, q)][:],
            )

        def spread_new_bias(all_ones):
            for i in range(U * H // BANK):
                acc = psum.tile([P, BANK], F32, name="bias_bank", tag="bank")
                nc.tensor.matmul(
                    out=acc[:], lhsT=all_ones, rhs=bias_new_rows[:, BANK * i : BANK * (i + 1)], start=True, stop=True
                )
                nc.scalar.copy(out=bias_new_sb[:, BANK * i : BANK * (i + 1)], in_=acc[:])

        def idle_matmuls(all_ones, count):
            acc = psum.tile([P, BANK], F32, name="idle_bank", tag="bank")
            for i in range(count):
                nc.tensor.matmul(out=acc[:], lhsT=all_ones, rhs=bias_rows[:, 0:BANK], start=True, stop=True)

        def warm_up():
            late_bytes = (planes[1][:, 0, 0:64], planes[1][0:32, 4, 0:64], planes[1][32:64, 4, 0:64])
            probes = (probe[:, 0:16], probe[0:32, 16:32], probe[32:64, 32:48])
            for i in range(WARM_STEPS):
                nc.gpsimd.tensor_copy(out=probes[i], in_=late_bytes[i].bitcast(I32))
                nc.gpsimd.tensor_copy(out=late_ones[i][:], in_=ones[:])
            idle_matmuls(late_ones[0][:], 3)
            spread_new_bias(late_ones[1][:])
            idle_matmuls(late_ones[2][:], 2)

        for s in range(2 * PAIR_BLOCKS):
            transpose_two(0, s)
        for c in range(W_CHUNKS):
            multiply_w_chunk(c)
            if c == 0:
                load_the_rest()
            step = c - X_AFTER_CHUNK
            if step >= 0:
                transpose_inputs(step // 2, step % 2)
            if step >= 1:
                quantise_inputs((step - 1) // 2, (step - 1) % 2)
        quantise_inputs(U - 1, 1)
        warm_up()

        def mx_pass(acc, u, g, words, first_col, width):
            nc.tensor.matmul_mx(
                out=acc,
                lhsT=x_codes[:, PASSES * u + g, :].bitcast(FP8X4),
                lhsT_scale=x_scales[:, PASSES * u + g, :],
                rhs=words.bitcast(FP4X4),
                rhs_scale=planes[u][:, g, first_col : first_col + width],
                start=(g == 0),
                stop=(g == PASSES - 1),
            )

        def multiply_group(u, group):
            first_col, n_cols = GROUPS[u][group][0:2]
            starts = list(range(0, n_cols - n_cols % BANK, BANK)) + list(range(n_cols - n_cols % BANK, n_cols, NARROW))
            pieces = []
            for start in starts:
                width = BANK if start + BANK <= n_cols else NARROW
                acc = psum.tile([P, BANK], F32, name="acc%d_%d" % (group, start), tag="bank")
                pieces.append((start, width, acc))
            for g in range(PASSES):
                tile_u8, place = words[u][group][g]
                for start, width, acc in pieces:
                    start_byte = 2 * (n_cols * place + start)
                    mx_pass(
                        acc[:, 0:width],
                        u,
                        g,
                        tile_u8[:, start_byte : start_byte + 2 * width],
                        first_col + start,
                        width,
                    )
            return pieces

        for u in range(U):
            gh_u = gh_sb[:, GATES * u : GATES * (u + 1)]
            gh_new = gh_u[:, 2 * H : 3 * H]
            bias_new = bias_new_sb[:, H * u : H * (u + 1)]
            pre = gate_pool.tile([P, 2 * H], F32, name="pre")
            gates = gate_pool.tile([P, 2 * H], F32, name="gates")
            keep_new = gate_pool.tile([P, H], F32, name="keep_new")
            cand = gate_pool.tile([P, H], F32, name="cand")
            old_part = gate_pool.tile([P, H], F32, name="old_part")
            result = gate_pool.tile([P, H], F32, name="result")

            def add_hidden_part(first_col, pieces):
                for start, width, acc in pieces:
                    cols = slice(first_col + start, first_col + start + width)
                    nc.vector.tensor_add(out=pre[:, cols], in0=acc[:, 0:width], in1=gh_u[:, cols])

            def sigmoid_part(lo, hi):
                nc.scalar.activation(out=gates[:, lo:hi], in_=pre[:, lo:hi], func=SIGMOID)

            def keep_new_part(lo, hi):
                nc.scalar.activation(out=keep_new[:, lo:hi], in_=pre[:, H + lo : H + hi], func=SIGMOID, scale=-1.0)

            def cand_part(lo, hi):
                nc.vector.tensor_mul(out=cand[:, lo:hi], in0=gates[:, lo:hi], in1=gh_new[:, lo:hi])

            def cand_bias_part(lo, hi):
                nc.vector.tensor_add(out=cand[:, lo:hi], in0=cand[:, lo:hi], in1=bias_new[:, lo:hi])

            def old_part_part(lo, hi):
                nc.vector.tensor_mul(out=old_part[:, lo:hi], in0=gates[:, H + lo : H + hi], in1=hidden_sb[:, u, lo:hi])

            def add_new_part(first_col, pieces):
                for start, width, acc in pieces:
                    cols = slice(first_col + start, first_col + start + width)
                    nc.vector.tensor_add(out=cand[:, cols], in0=acc[:, 0:width], in1=cand[:, cols])

            def tanh_part(lo, hi):
                nc.scalar.activation(out=cand[:, lo:hi], in_=cand[:, lo:hi], func=TANH)

            def blend_new_part(lo, hi):
                nc.vector.tensor_mul(out=result[:, lo:hi], in0=cand[:, lo:hi], in1=keep_new[:, lo:hi])

            def finish_part(lo, hi):
                nc.vector.tensor_add(out=result[:, lo:hi], in0=result[:, lo:hi], in1=old_part[:, lo:hi])
                nc.sync.dma_start(out=out[:, u, lo:hi], in_=result[:, lo:hi])

            if u == 0:
                pieces = multiply_group(u, 0)
                add_hidden_part(0, pieces)
                sigmoid_part(0, BANK)
                sigmoid_part(BANK, 2 * BANK)
                sigmoid_part(2 * BANK, 3 * BANK)
                keep_new_part(0, H)
                pieces = multiply_group(u, 1)
                cand_part(0, BANK)
                cand_part(BANK, H)
                cand_bias_part(0, H)
                add_new_part(0, pieces)
                tanh_part(0, BANK)
                tanh_part(BANK, H)
                old_part_part(0, H)
                blend_new_part(0, BANK)
                blend_new_part(BANK, H)
                finish_part(0, BANK)
                finish_part(BANK, H)
            else:
                split = 2 * BANK - H
                add_hidden_part(0, multiply_group(u, 0))
                sigmoid_part(0, BANK)
                sigmoid_part(BANK, 2 * BANK)
                keep_new_part(0, split)
                cand_part(0, BANK)
                cand_part(BANK, H)

                add_hidden_part(2 * BANK, multiply_group(u, 1))
                sigmoid_part(2 * BANK, 3 * BANK)
                keep_new_part(split, H)
                cand_bias_part(0, H)
                old_part_part(0, split)

                add_new_part(0, multiply_group(u, 2))
                tanh_part(0, BANK)
                old_part_part(split, H)

                add_new_part(BANK, multiply_group(u, 3))
                tanh_part(BANK, H)
                blend_new_part(0, BANK)
                finish_part(0, BANK)
                blend_new_part(BANK, H)
                finish_part(BANK, H)
